import numpy as np
import ml_dtypes

BF16 = ml_dtypes.bfloat16


def bf(x):
    return np.asarray(x, np.float32).astype(BF16)


def f32(x):
    return np.asarray(x, np.float32)


def f64(x):
    return np.asarray(x).astype(np.float64)


def striped(idx):
    return np.tile(idx.reshape(-1, 16).T, (8, 1))


D, S, N, E, F = 128, 512, 128, 4, 128
INDEX = 0
EDGES = (-0.5, 0.0, 0.5)
YMAX = 0.98


def setup_inputs():
    t = np.random.standard_normal((D, S))
    t[INDEX] = np.random.uniform(-YMAX, YMAX, S)
    return {"table": bf(t), "w": bf(np.random.standard_normal((D, E * F)) / np.sqrt(D)), "offs": striped(np.random.permutation(S)[:N])}


def reference(table, w, offs):
    idx = offs[:16].T.reshape(-1)
    g = f64(table)[:, idx]
    h = (f64(w).T @ g).reshape(E, F, N)
    y = g[INDEX]
    mem = np.zeros(N)
    for e in EDGES:
        mem = mem + (y > e).astype(np.float64)
    out = np.zeros((F, N))
    for k in range(E):
        out = out + (mem == k).astype(np.float64)[None, :] * h[k]
    return out

@@ -1,0 +1,53 @@
+import concourse.mybir as mybir
+
+BF16, F32, U16 = mybir.dt.bfloat16, mybir.dt.float32, mybir.dt.uint16
+ALU = mybir.AluOpType
+
+P = 128
+STORED = 512
+PICKED = 128
+EXPERTS = 4
+EDGES = (-0.5, 0.0, 0.5)
+
+FLOPS = 2 * P * EXPERTS * P * PICKED
+
+
+def tile_dispatchbyvariable_kernel(tc, table, w, offs, out):
+    nc = tc.nc
+    with (
+        tc.tile_pool(name="held", bufs=1) as held,
+        tc.psum_pool(name="psum", bufs=1) as psum,
+    ):
+        offsets = held.tile([P, PICKED // 16], U16, name="offsets")
+        nc.sync.dma_start(offsets[:], offs)
+        tokens = held.tile([P, STORED], BF16, name="tokens")
+        nc.scalar.dma_start(tokens[:], table)
+        weights = held.tile([P, EXPERTS * P], BF16, name="weights")
+        nc.sync.dma_start(weights[:], w)
+
+        pick_feature0 = held.tile([P, P], BF16, name="pick_feature0")
+        nc.vector.memset(pick_feature0[:], 0.0)
+        nc.vector.memset(pick_feature0[0:1, :], 1.0)
+
+        y = psum.tile([P, PICKED], F32, name="y")
+        nc.tensor.matmul(y[:], pick_feature0[:], tokens[:].indirect(offsets[:]), start=True, stop=True)
+
+        h = [psum.tile([P, PICKED], F32, name=f"h{k}") for k in range(EXPERTS)]
+        for k in range(EXPERTS):
+            nc.tensor.matmul(
+                h[k][:], weights[:, k * P : (k + 1) * P], tokens[:].indirect(offsets[:]), start=True, stop=True
+            )
+
+        bins = held.tile([P, PICKED], F32, name="bins")
+        nc.vector.tensor_single_scalar(bins[:], y[:], EDGES[0], op=ALU.is_gt)
+        for edge in EDGES[1:]:
+            nc.vector.scalar_tensor_tensor(bins[:], y[:], edge, bins[:], op0=ALU.is_gt, op1=ALU.add)
+
+        chosen = held.tile([P, PICKED], F32, name="chosen")
+        nc.vector.scalar_tensor_tensor(chosen[:], bins[:], 0.0, h[0][:], op0=ALU.is_equal, op1=ALU.mult)
+        for k in range(1, EXPERTS):
+            term = held.tile([P, PICKED], F32, name=f"term{k}")
+            nc.vector.scalar_tensor_tensor(term[:], bins[:], float(k), h[k][:], op0=ALU.is_equal, op1=ALU.mult)
+            nc.vector.tensor_add(chosen[:], chosen[:], term[:])
+
+        nc.sync.dma_start(out, chosen[:])

@@ -11,6 +11,8 @@ EDGES = (-0.5, 0.0, 0.5)
 
 FLOPS = 2 * P * EXPERTS * P * PICKED
 
+ORDER = (1, 2, 0, 3)
+
 
 def tile_dispatchbyvariable_kernel(tc, table, w, offs, out):
     nc = tc.nc
@@ -29,25 +31,28 @@ def tile_dispatchbyvariable_kernel(tc, table, w, offs, out):
         nc.vector.memset(pick_feature0[:], 0.0)
         nc.vector.memset(pick_feature0[0:1, :], 1.0)
 
-        y = psum.tile([P, PICKED], F32, name="y")
-        nc.tensor.matmul(y[:], pick_feature0[:], tokens[:].indirect(offsets[:]), start=True, stop=True)
+        y_psum = psum.tile([P, PICKED], F32, name="y_psum")
+        nc.tensor.matmul(y_psum[:], pick_feature0[:], tokens[:].indirect(offsets[:]), start=True, stop=True)
 
         h = [psum.tile([P, PICKED], F32, name=f"h{k}") for k in range(EXPERTS)]
-        for k in range(EXPERTS):
+        for k in ORDER:
             nc.tensor.matmul(
                 h[k][:], weights[:, k * P : (k + 1) * P], tokens[:].indirect(offsets[:]), start=True, stop=True
             )
 
-        bins = held.tile([P, PICKED], F32, name="bins")
-        nc.vector.tensor_single_scalar(bins[:], y[:], EDGES[0], op=ALU.is_gt)
-        for edge in EDGES[1:]:
-            nc.vector.scalar_tensor_tensor(bins[:], y[:], edge, bins[:], op0=ALU.is_gt, op1=ALU.add)
+        y = held.tile([P, PICKED], F32, name="y")
+        nc.scalar.copy(y[:], y_psum[:])
 
         chosen = held.tile([P, PICKED], F32, name="chosen")
-        nc.vector.scalar_tensor_tensor(chosen[:], bins[:], 0.0, h[0][:], op0=ALU.is_equal, op1=ALU.mult)
-        for k in range(1, EXPERTS):
-            term = held.tile([P, PICKED], F32, name=f"term{k}")
-            nc.vector.scalar_tensor_tensor(term[:], bins[:], float(k), h[k][:], op0=ALU.is_equal, op1=ALU.mult)
-            nc.vector.tensor_add(chosen[:], chosen[:], term[:])
+        for i, k in enumerate(ORDER):
+            term = chosen if i == 0 else held.tile([P, PICKED], F32, name=f"term{k}")
+            bounded = h[k]
+            if k > 0:
+                nc.vector.scalar_tensor_tensor(term[:], y[:], EDGES[k - 1], bounded[:], op0=ALU.is_gt, op1=ALU.mult)
+                bounded = term
+            if k < EXPERTS - 1:
+                nc.vector.scalar_tensor_tensor(term[:], y[:], EDGES[k], bounded[:], op0=ALU.is_le, op1=ALU.mult)
+            if i > 0:
+                nc.vector.tensor_add(chosen[:], chosen[:], term[:])
 
         nc.sync.dma_start(out, chosen[:])

@@ -13,6 +13,9 @@ FLOPS = 2 * P * EXPERTS * P * PICKED
 
 ORDER = (1, 2, 0, 3)
 
+WARM_MATMULS = 4
+WARM_COLUMNS = 512
+
 
 def tile_dispatchbyvariable_kernel(tc, table, w, offs, out):
     nc = tc.nc
@@ -30,6 +33,12 @@ def tile_dispatchbyvariable_kernel(tc, table, w, offs, out):
         pick_feature0 = held.tile([P, P], BF16, name="pick_feature0")
         nc.vector.memset(pick_feature0[:], 0.0)
         nc.vector.memset(pick_feature0[0:1, :], 1.0)
+
+        zeros = held.tile([P, WARM_COLUMNS], BF16, name="zeros")
+        nc.gpsimd.memset(zeros[:], 0.0)
+        warm = psum.tile([P, WARM_COLUMNS], F32, name="warm")
+        for i in range(WARM_MATMULS):
+            nc.tensor.matmul(warm[:], zeros[:, 0:P], zeros[:], start=True, stop=True)
 
         y_psum = psum.tile([P, PICKED], F32, name="y_psum")
         nc.tensor.matmul(y_psum[:], pick_feature0[:], tokens[:].indirect(offsets[:]), start=True, stop=True)

@@ -12,9 +12,7 @@ EDGES = (-0.5, 0.0, 0.5)
 FLOPS = 2 * P * EXPERTS * P * PICKED
 
 ORDER = (1, 2, 0, 3)
-
-WARM_MATMULS = 4
-WARM_COLUMNS = 512
+HALF = STORED // 2
 
 
 def tile_dispatchbyvariable_kernel(tc, table, w, offs, out):
@@ -26,19 +24,14 @@ def tile_dispatchbyvariable_kernel(tc, table, w, offs, out):
         offsets = held.tile([P, PICKED // 16], U16, name="offsets")
         nc.sync.dma_start(offsets[:], offs)
         tokens = held.tile([P, STORED], BF16, name="tokens")
-        nc.scalar.dma_start(tokens[:], table)
         weights = held.tile([P, EXPERTS * P], BF16, name="weights")
-        nc.sync.dma_start(weights[:], w)
+        for tile, source in ((tokens, table), (weights, w)):
+            nc.sync.dma_start(tile[:, 0:HALF], source[:, 0:HALF])
+            nc.scalar.dma_start(tile[:, HALF:], source[:, HALF:])
 
         pick_feature0 = held.tile([P, P], BF16, name="pick_feature0")
         nc.vector.memset(pick_feature0[:], 0.0)
         nc.vector.memset(pick_feature0[0:1, :], 1.0)
-
-        zeros = held.tile([P, WARM_COLUMNS], BF16, name="zeros")
-        nc.gpsimd.memset(zeros[:], 0.0)
-        warm = psum.tile([P, WARM_COLUMNS], F32, name="warm")
-        for i in range(WARM_MATMULS):
-            nc.tensor.matmul(warm[:], zeros[:, 0:P], zeros[:], start=True, stop=True)
 
         y_psum = psum.tile([P, PICKED], F32, name="y_psum")
         nc.tensor.matmul(y_psum[:], pick_feature0[:], tokens[:].indirect(offsets[:]), start=True, stop=True)

@@ -12,6 +12,8 @@ EDGES = (-0.5, 0.0, 0.5)
 FLOPS = 2 * P * EXPERTS * P * PICKED
 
 ORDER = (1, 2, 0, 3)
+WARM_MATMULS = 3
+WARM_COLUMNS = 512
 HALF = STORED // 2
 
 
@@ -28,6 +30,12 @@ def tile_dispatchbyvariable_kernel(tc, table, w, offs, out):
         for tile, source in ((tokens, table), (weights, w)):
             nc.sync.dma_start(tile[:, 0:HALF], source[:, 0:HALF])
             nc.scalar.dma_start(tile[:, HALF:], source[:, HALF:])
+
+        zeros = held.tile([P, WARM_COLUMNS], BF16, name="zeros")
+        nc.vector.memset(zeros[:], 0.0)
+        warm = psum.tile([P, WARM_COLUMNS], F32, name="warm")
+        for i in range(WARM_MATMULS):
+            nc.tensor.matmul(warm[:], zeros[:, 0:P], zeros[:], start=True, stop=True)
 
         pick_feature0 = held.tile([P, P], BF16, name="pick_feature0")
         nc.vector.memset(pick_feature0[:], 0.0)

@@ -12,8 +12,6 @@ EDGES = (-0.5, 0.0, 0.5)
 FLOPS = 2 * P * EXPERTS * P * PICKED
 
 ORDER = (1, 2, 0, 3)
-WARM_MATMULS = 3
-WARM_COLUMNS = 512
 HALF = STORED // 2
 
 
@@ -31,12 +29,6 @@ def tile_dispatchbyvariable_kernel(tc, table, w, offs, out):
             nc.sync.dma_start(tile[:, 0:HALF], source[:, 0:HALF])
             nc.scalar.dma_start(tile[:, HALF:], source[:, HALF:])
 
-        zeros = held.tile([P, WARM_COLUMNS], BF16, name="zeros")
-        nc.vector.memset(zeros[:], 0.0)
-        warm = psum.tile([P, WARM_COLUMNS], F32, name="warm")
-        for i in range(WARM_MATMULS):
-            nc.tensor.matmul(warm[:], zeros[:, 0:P], zeros[:], start=True, stop=True)
-
         pick_feature0 = held.tile([P, P], BF16, name="pick_feature0")
         nc.vector.memset(pick_feature0[:], 0.0)
         nc.vector.memset(pick_feature0[0:1, :], 1.0)
@@ -51,7 +43,7 @@ def tile_dispatchbyvariable_kernel(tc, table, w, offs, out):
             )
 
         y = held.tile([P, PICKED], F32, name="y")
-        nc.scalar.copy(y[:], y_psum[:])
+        nc.vector.tensor_copy(y[:], y_psum[:])
 
         chosen = held.tile([P, PICKED], F32, name="chosen")
         for i, k in enumerate(ORDER):

@@ -11,8 +11,8 @@ EDGES = (-0.5, 0.0, 0.5)
 
 FLOPS = 2 * P * EXPERTS * P * PICKED
 
-ORDER = (1, 2, 0, 3)
 HALF = STORED // 2
+ORDER = (1, 2, 0, 3)
 
 
 def tile_dispatchbyvariable_kernel(tc, table, w, offs, out):
@@ -43,18 +43,25 @@ def tile_dispatchbyvariable_kernel(tc, table, w, offs, out):
             )
 
         y = held.tile([P, PICKED], F32, name="y")
-        nc.vector.tensor_copy(y[:], y_psum[:])
+        nc.scalar.copy(y[:], y_psum[:])
 
+        term = [held.tile([P, PICKED], F32, name=f"term{k}") for k in range(EXPERTS)]
         chosen = held.tile([P, PICKED], F32, name="chosen")
-        for i, k in enumerate(ORDER):
-            term = chosen if i == 0 else held.tile([P, PICKED], F32, name=f"term{k}")
-            bounded = h[k]
-            if k > 0:
-                nc.vector.scalar_tensor_tensor(term[:], y[:], EDGES[k - 1], bounded[:], op0=ALU.is_gt, op1=ALU.mult)
-                bounded = term
-            if k < EXPERTS - 1:
-                nc.vector.scalar_tensor_tensor(term[:], y[:], EDGES[k], bounded[:], op0=ALU.is_le, op1=ALU.mult)
-            if i > 0:
-                nc.vector.tensor_add(chosen[:], chosen[:], term[:])
+
+        def keep_above(k, source):
+            nc.vector.scalar_tensor_tensor(term[k][:], y[:], EDGES[k - 1], source[:], op0=ALU.is_gt, op1=ALU.mult)
+
+        def keep_up_to(k, source):
+            nc.vector.scalar_tensor_tensor(term[k][:], y[:], EDGES[k], source[:], op0=ALU.is_le, op1=ALU.mult)
+
+        keep_above(1, h[1])
+        keep_above(2, h[2])
+        keep_up_to(1, term[1])
+        keep_up_to(2, term[2])
+        keep_up_to(0, h[0])
+        nc.vector.tensor_add(chosen[:], term[1][:], term[2][:])
+        keep_above(3, h[3])
+        nc.vector.tensor_add(chosen[:], chosen[:], term[0][:])
+        nc.vector.tensor_add(chosen[:], chosen[:], term[3][:])
 
         nc.sync.dma_start(out, chosen[:])

@@ -5,14 +5,15 @@ ALU = mybir.AluOpType
 
 P = 128
 STORED = 512
+HALF = STORED // 2
 PICKED = 128
 EXPERTS = 4
 EDGES = (-0.5, 0.0, 0.5)
+MIDDLE = (1, 2)
+OUTER = (0, 3)
+ORDER = MIDDLE + OUTER
 
 FLOPS = 2 * P * EXPERTS * P * PICKED
-
-HALF = STORED // 2
-ORDER = (1, 2, 0, 3)
 
 
 def tile_dispatchbyvariable_kernel(tc, table, w, offs, out):
@@ -24,10 +25,12 @@ def tile_dispatchbyvariable_kernel(tc, table, w, offs, out):
         offsets = held.tile([P, PICKED // 16], U16, name="offsets")
         nc.sync.dma_start(offsets[:], offs)
         tokens = held.tile([P, STORED], BF16, name="tokens")
+        nc.scalar.dma_start(tokens[:, 0:HALF], table[:, 0:HALF])
+        nc.sync.dma_start(tokens[:, HALF:], table[:, HALF:])
         weights = held.tile([P, EXPERTS * P], BF16, name="weights")
-        for tile, source in ((tokens, table), (weights, w)):
-            nc.sync.dma_start(tile[:, 0:HALF], source[:, 0:HALF])
-            nc.scalar.dma_start(tile[:, HALF:], source[:, HALF:])
+        nc.scalar.dma_start(weights[:, P : 3 * P], w[:, P : 3 * P])
+        nc.sync.dma_start(weights[:, 0:P], w[:, 0:P])
+        nc.scalar.dma_start(weights[:, 3 * P :], w[:, 3 * P :])
 
         pick_feature0 = held.tile([P, P], BF16, name="pick_feature0")
         nc.vector.memset(pick_feature0[:], 0.0)
@@ -46,22 +49,18 @@ def tile_dispatchbyvariable_kernel(tc, table, w, offs, out):
         nc.scalar.copy(y[:], y_psum[:])
 
         term = [held.tile([P, PICKED], F32, name=f"term{k}") for k in range(EXPERTS)]
+        for k in MIDDLE:
+            nc.vector.scalar_tensor_tensor(term[k][:], y[:], EDGES[k - 1], h[k][:], op0=ALU.is_gt, op1=ALU.mult)
+        for k in MIDDLE:
+            nc.vector.scalar_tensor_tensor(term[k][:], y[:], EDGES[k], term[k][:], op0=ALU.is_le, op1=ALU.mult)
+        nc.vector.scalar_tensor_tensor(term[0][:], y[:], EDGES[0], h[0][:], op0=ALU.is_le, op1=ALU.mult)
+        nc.vector.scalar_tensor_tensor(term[3][:], y[:], EDGES[2], h[3][:], op0=ALU.is_gt, op1=ALU.mult)
+
+        middle = held.tile([P, PICKED], F32, name="middle")
+        nc.vector.tensor_add(middle[:], term[1][:], term[2][:])
+        outer = held.tile([P, PICKED], F32, name="outer")
+        nc.vector.tensor_add(outer[:], term[0][:], term[3][:])
         chosen = held.tile([P, PICKED], F32, name="chosen")
-
-        def keep_above(k, source):
-            nc.vector.scalar_tensor_tensor(term[k][:], y[:], EDGES[k - 1], source[:], op0=ALU.is_gt, op1=ALU.mult)
-
-        def keep_up_to(k, source):
-            nc.vector.scalar_tensor_tensor(term[k][:], y[:], EDGES[k], source[:], op0=ALU.is_le, op1=ALU.mult)
-
-        keep_above(1, h[1])
-        keep_above(2, h[2])
-        keep_up_to(1, term[1])
-        keep_up_to(2, term[2])
-        keep_up_to(0, h[0])
-        nc.vector.tensor_add(chosen[:], term[1][:], term[2][:])
-        keep_above(3, h[3])
-        nc.vector.tensor_add(chosen[:], chosen[:], term[0][:])
-        nc.vector.tensor_add(chosen[:], chosen[:], term[3][:])
+        nc.vector.tensor_add(chosen[:], middle[:], outer[:])
 
         nc.sync.dma_start(out, chosen[:])

@@ -9,9 +9,11 @@ HALF = STORED // 2
 PICKED = 128
 EXPERTS = 4
 EDGES = (-0.5, 0.0, 0.5)
-MIDDLE = (1, 2)
 OUTER = (0, 3)
-ORDER = MIDDLE + OUTER
+MIDDLE = (1, 2)
+QUARTER = 32
+ONES_ROW = 3 * QUARTER
+FAR = 2.0**126
 
 FLOPS = 2 * P * EXPERTS * P * PICKED
 
@@ -28,39 +30,54 @@ def tile_dispatchbyvariable_kernel(tc, table, w, offs, out):
         nc.scalar.dma_start(tokens[:, 0:HALF], table[:, 0:HALF])
         nc.sync.dma_start(tokens[:, HALF:], table[:, HALF:])
         weights = held.tile([P, EXPERTS * P], BF16, name="weights")
+        nc.scalar.dma_start(weights[:, 0:P], w[:, 0:P])
+        nc.sync.dma_start(weights[:, 3 * P :], w[:, 3 * P :])
         nc.scalar.dma_start(weights[:, P : 3 * P], w[:, P : 3 * P])
-        nc.sync.dma_start(weights[:, 0:P], w[:, 0:P])
-        nc.scalar.dma_start(weights[:, 3 * P :], w[:, 3 * P :])
 
         pick_feature0 = held.tile([P, P], BF16, name="pick_feature0")
         nc.vector.memset(pick_feature0[:], 0.0)
         nc.vector.memset(pick_feature0[0:1, :], 1.0)
 
+        edge = held.tile([P, 1], F32, name="edge")
+        for i in range(len(EDGES)):
+            nc.vector.memset(edge[i * QUARTER : (i + 1) * QUARTER, :], EDGES[i])
+        above = held.tile([P, PICKED], BF16, name="above")
+        nc.vector.memset(above[ONES_ROW:, :], 1.0)
+
+        bar_weights = held.tile([P, EXPERTS * P], BF16, name="bar_weights")
+        nc.vector.memset(bar_weights[:], 0.0)
+        for k in MIDDLE:
+            columns = slice(k * P, (k + 1) * P)
+            nc.vector.memset(bar_weights[ONES_ROW : ONES_ROW + 1, columns], -FAR)
+            nc.vector.memset(bar_weights[(k - 1) * QUARTER : (k - 1) * QUARTER + 1, columns], FAR)
+            nc.vector.memset(bar_weights[k * QUARTER : k * QUARTER + 1, columns], -FAR)
+
         y_psum = psum.tile([P, PICKED], F32, name="y_psum")
         nc.tensor.matmul(y_psum[:], pick_feature0[:], tokens[:].indirect(offsets[:]), start=True, stop=True)
 
         h = [psum.tile([P, PICKED], F32, name=f"h{k}") for k in range(EXPERTS)]
-        for k in ORDER:
+        for k in OUTER + MIDDLE:
             nc.tensor.matmul(
-                h[k][:], weights[:, k * P : (k + 1) * P], tokens[:].indirect(offsets[:]), start=True, stop=True
+                h[k][:], weights[:, k * P : (k + 1) * P], tokens[:].indirect(offsets[:]), start=True, stop=(k in OUTER)
             )
 
-        y = held.tile([P, PICKED], F32, name="y")
-        nc.scalar.copy(y[:], y_psum[:])
+        nc.vector.tensor_scalar(
+            above[0:ONES_ROW, :], y_psum[0:ONES_ROW, :], edge[0:ONES_ROW, :], None, op0=ALU.is_gt
+        )
+        bar = {k: held.tile([P, PICKED], F32, name=f"bar{k}") for k in OUTER}
+        nc.vector.tensor_scalar(bar[0][:], y_psum[:], EDGES[0], -FAR, op0=ALU.is_gt, op1=ALU.mult)
+        nc.vector.tensor_scalar(bar[3][:], y_psum[:], EDGES[2], -FAR, op0=ALU.is_le, op1=ALU.mult)
+        barred = {k: held.tile([P, PICKED], F32, name=f"barred{k}") for k in OUTER}
+        for k in OUTER:
+            nc.vector.tensor_tensor(barred[k][:], h[k][:], bar[k][:], op=ALU.add)
 
-        term = [held.tile([P, PICKED], F32, name=f"term{k}") for k in range(EXPERTS)]
         for k in MIDDLE:
-            nc.vector.scalar_tensor_tensor(term[k][:], y[:], EDGES[k - 1], h[k][:], op0=ALU.is_gt, op1=ALU.mult)
-        for k in MIDDLE:
-            nc.vector.scalar_tensor_tensor(term[k][:], y[:], EDGES[k], term[k][:], op0=ALU.is_le, op1=ALU.mult)
-        nc.vector.scalar_tensor_tensor(term[0][:], y[:], EDGES[0], h[0][:], op0=ALU.is_le, op1=ALU.mult)
-        nc.vector.scalar_tensor_tensor(term[3][:], y[:], EDGES[2], h[3][:], op0=ALU.is_gt, op1=ALU.mult)
+            nc.tensor.matmul(h[k][:], bar_weights[:, k * P : (k + 1) * P], above[:], start=False, stop=True)
 
-        middle = held.tile([P, PICKED], F32, name="middle")
-        nc.vector.tensor_add(middle[:], term[1][:], term[2][:])
-        outer = held.tile([P, PICKED], F32, name="outer")
-        nc.vector.tensor_add(outer[:], term[0][:], term[3][:])
+        pair = [held.tile([P, PICKED], F32, name=f"pair{i}") for i in range(2)]
+        for i in range(2):
+            nc.vector.tensor_tensor(pair[i][:], h[MIDDLE[i]][:], barred[OUTER[i]][:], op=ALU.max)
         chosen = held.tile([P, PICKED], F32, name="chosen")
-        nc.vector.tensor_add(chosen[:], middle[:], outer[:])
+        nc.vector.tensor_tensor(chosen[:], pair[0][:], pair[1][:], op=ALU.max)
 
         nc.sync.dma_start(out, chosen[:])

@@ -61,12 +61,12 @@ def tile_dispatchbyvariable_kernel(tc, table, w, offs, out):
                 h[k][:], weights[:, k * P : (k + 1) * P], tokens[:].indirect(offsets[:]), start=True, stop=(k in OUTER)
             )
 
-        nc.vector.tensor_scalar(
-            above[0:ONES_ROW, :], y_psum[0:ONES_ROW, :], edge[0:ONES_ROW, :], None, op0=ALU.is_gt
-        )
         bar = {k: held.tile([P, PICKED], F32, name=f"bar{k}") for k in OUTER}
         nc.vector.tensor_scalar(bar[0][:], y_psum[:], EDGES[0], -FAR, op0=ALU.is_gt, op1=ALU.mult)
         nc.vector.tensor_scalar(bar[3][:], y_psum[:], EDGES[2], -FAR, op0=ALU.is_le, op1=ALU.mult)
+        nc.vector.tensor_scalar(
+            above[0:ONES_ROW, :], y_psum[0:ONES_ROW, :], edge[0:ONES_ROW, :], None, op0=ALU.is_gt
+        )
         barred = {k: held.tile([P, PICKED], F32, name=f"barred{k}") for k in OUTER}
         for k in OUTER:
             nc.vector.tensor_tensor(barred[k][:], h[k][:], bar[k][:], op=ALU.add)

@@ -5,7 +5,6 @@ ALU = mybir.AluOpType
 
 P = 128
 STORED = 512
-HALF = STORED // 2
 PICKED = 128
 EXPERTS = 4
 EDGES = (-0.5, 0.0, 0.5)
@@ -27,12 +26,9 @@ def tile_dispatchbyvariable_kernel(tc, table, w, offs, out):
         offsets = held.tile([P, PICKED // 16], U16, name="offsets")
         nc.sync.dma_start(offsets[:], offs)
         tokens = held.tile([P, STORED], BF16, name="tokens")
-        nc.scalar.dma_start(tokens[:, 0:HALF], table[:, 0:HALF])
-        nc.sync.dma_start(tokens[:, HALF:], table[:, HALF:])
+        nc.sync.dma_start(tokens[:], table)
         weights = held.tile([P, EXPERTS * P], BF16, name="weights")
-        nc.scalar.dma_start(weights[:, 0:P], w[:, 0:P])
-        nc.sync.dma_start(weights[:, 3 * P :], w[:, 3 * P :])
-        nc.scalar.dma_start(weights[:, P : 3 * P], w[:, P : 3 * P])
+        nc.sync.dma_start(weights[:], w)
 
         pick_feature0 = held.tile([P, P], BF16, name="pick_feature0")
         nc.vector.memset(pick_feature0[:], 0.0)

@@ -40,13 +40,12 @@ def tile_dispatchbyvariable_kernel(tc, table, w, offs, out):
         above = held.tile([P, PICKED], BF16, name="above")
         nc.vector.memset(above[ONES_ROW:, :], 1.0)
 
-        bar_weights = held.tile([P, EXPERTS * P], BF16, name="bar_weights")
-        nc.vector.memset(bar_weights[:], 0.0)
+        bar_weights = {k: held.tile([P, P], BF16, name=f"bar_weights{k}") for k in MIDDLE}
         for k in MIDDLE:
-            columns = slice(k * P, (k + 1) * P)
-            nc.vector.memset(bar_weights[ONES_ROW : ONES_ROW + 1, columns], -FAR)
-            nc.vector.memset(bar_weights[(k - 1) * QUARTER : (k - 1) * QUARTER + 1, columns], FAR)
-            nc.vector.memset(bar_weights[k * QUARTER : k * QUARTER + 1, columns], -FAR)
+            nc.vector.memset(bar_weights[k][:], 0.0)
+            nc.vector.memset(bar_weights[k][ONES_ROW : ONES_ROW + 1, :], -FAR)
+            nc.vector.memset(bar_weights[k][(k - 1) * QUARTER : (k - 1) * QUARTER + 1, :], FAR)
+            nc.vector.memset(bar_weights[k][k * QUARTER : k * QUARTER + 1, :], -FAR)
 
         y_psum = psum.tile([P, PICKED], F32, name="y_psum")
         nc.tensor.matmul(y_psum[:], pick_feature0[:], tokens[:].indirect(offsets[:]), start=True, stop=True)
@@ -68,7 +67,7 @@ def tile_dispatchbyvariable_kernel(tc, table, w, offs, out):
             nc.vector.tensor_tensor(barred[k][:], h[k][:], bar[k][:], op=ALU.add)
 
         for k in MIDDLE:
-            nc.tensor.matmul(h[k][:], bar_weights[:, k * P : (k + 1) * P], above[:], start=False, stop=True)
+            nc.tensor.matmul(h[k][:], bar_weights[k][:], above[:], start=False, stop=True)
 
         pair = [held.tile([P, PICKED], F32, name=f"pair{i}") for i in range(2)]
         for i in range(2):

@@ -23,10 +23,10 @@ def tile_dispatchbyvariable_kernel(tc, table, w, offs, out):
         tc.tile_pool(name="held", bufs=1) as held,
         tc.psum_pool(name="psum", bufs=1) as psum,
     ):
-        offsets = held.tile([P, PICKED // 16], U16, name="offsets")
-        nc.sync.dma_start(offsets[:], offs)
         tokens = held.tile([P, STORED], BF16, name="tokens")
         nc.sync.dma_start(tokens[:], table)
+        offsets = held.tile([P, PICKED // 16], U16, name="offsets")
+        nc.sync.dma_start(offsets[:], offs)
         weights = held.tile([P, EXPERTS * P], BF16, name="weights")
         nc.sync.dma_start(weights[:], w)
 

@@ -42,10 +42,10 @@ def tile_dispatchbyvariable_kernel(tc, table, w, offs, out):
 
         bar_weights = {k: held.tile([P, P], BF16, name=f"bar_weights{k}") for k in MIDDLE}
         for k in MIDDLE:
-            nc.vector.memset(bar_weights[k][:], 0.0)
-            nc.vector.memset(bar_weights[k][ONES_ROW : ONES_ROW + 1, :], -FAR)
-            nc.vector.memset(bar_weights[k][(k - 1) * QUARTER : (k - 1) * QUARTER + 1, :], FAR)
-            nc.vector.memset(bar_weights[k][k * QUARTER : k * QUARTER + 1, :], -FAR)
+            nc.gpsimd.memset(bar_weights[k][:], 0.0)
+            nc.gpsimd.memset(bar_weights[k][ONES_ROW : ONES_ROW + 1, :], -FAR)
+            nc.gpsimd.memset(bar_weights[k][(k - 1) * QUARTER : (k - 1) * QUARTER + 1, :], FAR)
+            nc.gpsimd.memset(bar_weights[k][k * QUARTER : k * QUARTER + 1, :], -FAR)
 
         y_psum = psum.tile([P, PICKED], F32, name="y_psum")
         nc.tensor.matmul(y_psum[:], pick_feature0[:], tokens[:].indirect(offsets[:]), start=True, stop=True)

@@ -70,9 +70,14 @@ def tile_dispatchbyvariable_kernel(tc, table, w, offs, out):
             nc.tensor.matmul(h[k][:], bar_weights[k][:], above[:], start=False, stop=True)
 
         pair = [held.tile([P, PICKED], F32, name=f"pair{i}") for i in range(2)]
-        for i in range(2):
-            nc.vector.tensor_tensor(pair[i][:], h[MIDDLE[i]][:], barred[OUTER[i]][:], op=ALU.max)
+        halves = (slice(0, PICKED // 2), slice(PICKED // 2, PICKED))
+        for half in halves:
+            for i in range(2):
+                nc.vector.tensor_tensor(
+                    pair[i][:, half], h[MIDDLE[i]][:, half], barred[OUTER[i]][:, half], op=ALU.max
+                )
         chosen = held.tile([P, PICKED], F32, name="chosen")
-        nc.vector.tensor_tensor(chosen[:], pair[0][:], pair[1][:], op=ALU.max)
+        for half in halves:
+            nc.vector.tensor_tensor(chosen[:, half], pair[0][:, half], pair[1][:, half], op=ALU.max)
 
         nc.sync.dma_start(out, chosen[:])

@@ -10,6 +10,7 @@ EXPERTS = 4
 EDGES = (-0.5, 0.0, 0.5)
 OUTER = (0, 3)
 MIDDLE = (1, 2)
+DMA_BLOCK = 256
 QUARTER = 32
 ONES_ROW = 3 * QUARTER
 FAR = 2.0**126
@@ -23,11 +24,11 @@ def tile_dispatchbyvariable_kernel(tc, table, w, offs, out):
         tc.tile_pool(name="held", bufs=1) as held,
         tc.psum_pool(name="psum", bufs=1) as psum,
     ):
-        tokens = held.tile([P, STORED], BF16, name="tokens")
+        tokens = held.tile([P, STORED], BF16, name="tokens", align_bytes=DMA_BLOCK)
         nc.sync.dma_start(tokens[:], table)
         offsets = held.tile([P, PICKED // 16], U16, name="offsets")
         nc.sync.dma_start(offsets[:], offs)
-        weights = held.tile([P, EXPERTS * P], BF16, name="weights")
+        weights = held.tile([P, EXPERTS * P], BF16, name="weights", align_bytes=DMA_BLOCK)
         nc.sync.dma_start(weights[:], w)
 
         pick_feature0 = held.tile([P, P], BF16, name="pick_feature0")
@@ -76,7 +77,7 @@ def tile_dispatchbyvariable_kernel(tc, table, w, offs, out):
                 nc.vector.tensor_tensor(
                     pair[i][:, half], h[MIDDLE[i]][:, half], barred[OUTER[i]][:, half], op=ALU.max
                 )
-        chosen = held.tile([P, PICKED], F32, name="chosen")
+        chosen = held.tile([P, PICKED], F32, name="chosen", align_bytes=DMA_BLOCK)
         for half in halves:
             nc.vector.tensor_tensor(chosen[:, half], pair[0][:, half], pair[1][:, half], op=ALU.max)
 

import concourse.mybir as mybir

BF16, F32, U16 = mybir.dt.bfloat16, mybir.dt.float32, mybir.dt.uint16
ALU = mybir.AluOpType

P = 128
STORED = 512
PICKED = 128
EXPERTS = 4
EDGES = (-0.5, 0.0, 0.5)
OUTER = (0, 3)
MIDDLE = (1, 2)
DMA_BLOCK = 256
QUARTER = 32
ONES_ROW = 3 * QUARTER
FAR = 2.0**126

FLOPS = 2 * P * EXPERTS * P * PICKED


def tile_dispatchbyvariable_kernel(tc, table, w, offs, out):
    nc = tc.nc
    with (
        tc.tile_pool(name="held", bufs=1) as held,
        tc.psum_pool(name="psum", bufs=1) as psum,
    ):
        tokens = held.tile([P, STORED], BF16, name="tokens", align_bytes=DMA_BLOCK)
        nc.sync.dma_start(tokens[:], table)
        offsets = held.tile([P, PICKED // 16], U16, name="offsets")
        nc.sync.dma_start(offsets[:], offs)
        weights = held.tile([P, EXPERTS * P], BF16, name="weights", align_bytes=DMA_BLOCK)
        nc.sync.dma_start(weights[:], w)

        pick_feature0 = held.tile([P, P], BF16, name="pick_feature0")
        nc.vector.memset(pick_feature0[:], 0.0)
        nc.vector.memset(pick_feature0[0:1, :], 1.0)

        edge = held.tile([P, 1], F32, name="edge")
        for i in range(len(EDGES)):
            nc.vector.memset(edge[i * QUARTER : (i + 1) * QUARTER, :], EDGES[i])
        above = held.tile([P, PICKED], BF16, name="above")
        nc.vector.memset(above[ONES_ROW:, :], 1.0)

        bar_weights = {k: held.tile([P, P], BF16, name=f"bar_weights{k}") for k in MIDDLE}
        for k in MIDDLE:
            nc.gpsimd.memset(bar_weights[k][:], 0.0)
            nc.gpsimd.memset(bar_weights[k][ONES_ROW : ONES_ROW + 1, :], -FAR)
            nc.gpsimd.memset(bar_weights[k][(k - 1) * QUARTER : (k - 1) * QUARTER + 1, :], FAR)
            nc.gpsimd.memset(bar_weights[k][k * QUARTER : k * QUARTER + 1, :], -FAR)

        y_psum = psum.tile([P, PICKED], F32, name="y_psum")
        nc.tensor.matmul(y_psum[:], pick_feature0[:], tokens[:].indirect(offsets[:]), start=True, stop=True)

        h = [psum.tile([P, PICKED], F32, name=f"h{k}") for k in range(EXPERTS)]
        for k in OUTER + MIDDLE:
            nc.tensor.matmul(
                h[k][:], weights[:, k * P : (k + 1) * P], tokens[:].indirect(offsets[:]), start=True, stop=(k in OUTER)
            )

        bar = {k: held.tile([P, PICKED], F32, name=f"bar{k}") for k in OUTER}
        nc.vector.tensor_scalar(bar[0][:], y_psum[:], EDGES[0], -FAR, op0=ALU.is_gt, op1=ALU.mult)
        nc.vector.tensor_scalar(bar[3][:], y_psum[:], EDGES[2], -FAR, op0=ALU.is_le, op1=ALU.mult)
        nc.vector.tensor_scalar(
            above[0:ONES_ROW, :], y_psum[0:ONES_ROW, :], edge[0:ONES_ROW, :], None, op0=ALU.is_gt
        )
        barred = {k: held.tile([P, PICKED], F32, name=f"barred{k}") for k in OUTER}
        for k in OUTER:
            nc.vector.tensor_tensor(barred[k][:], h[k][:], bar[k][:], op=ALU.add)

        for k in MIDDLE:
            nc.tensor.matmul(h[k][:], bar_weights[k][:], above[:], start=False, stop=True)

        pair = [held.tile([P, PICKED], F32, name=f"pair{i}") for i in range(2)]
        halves = (slice(0, PICKED // 2), slice(PICKED // 2, PICKED))
        for half in halves:
            for i in range(2):
                nc.vector.tensor_tensor(
                    pair[i][:, half], h[MIDDLE[i]][:, half], barred[OUTER[i]][:, half], op=ALU.max
                )
        chosen = held.tile([P, PICKED], F32, name="chosen", align_bytes=DMA_BLOCK)
        for half in halves:
            nc.vector.tensor_tensor(chosen[:, half], pair[0][:, half], pair[1][:, half], op=ALU.max)

        nc.sync.dma_start(out, chosen[:])
